import numpy as np
import ml_dtypes


def mxq(x, axis, fmt="e4m3"):
    dtype, down = {"e4m3": (ml_dtypes.float8_e4m3fn, 7), "e5m2": (ml_dtypes.float8_e5m2, 14)}[fmt]
    v = np.moveaxis(np.asarray(x, np.float32).astype(ml_dtypes.bfloat16).astype(np.float64), axis, -1)
    blocks = v.reshape(v.shape[:-1] + (-1, 32))
    amax = np.abs(blocks).max(-1, keepdims=True)
    byte = np.maximum(np.where(amax > 0, np.frexp(amax)[1] - 1 + 127, 0) - down, 1)
    scale = np.exp2(byte - 127.0)
    codes = (blocks / scale).astype(np.float32).astype(dtype).astype(np.float64)
    return np.moveaxis((codes * scale).reshape(v.shape), -1, axis)


WIDE = False


def mx_kscale(k):
    if not WIDE:
        return np.ones(k)
    levels = np.array([10, -10, 5, -5, 0])
    a = np.random.permutation(np.resize(levels, k // 512 * 4)).reshape(k // 512, 4)
    idx = np.arange(k)
    return np.exp2(a[idx // 512, idx % 128 // 32])


BF16 = ml_dtypes.bfloat16


def bf(x):
    return np.asarray(x, np.float32).astype(BF16)


def f64(x):
    return np.asarray(x).astype(np.float64)


E2M1 = np.array([0.0, 0.5, 1.0, 1.5, 2.0, 3.0, 4.0, 6.0, -0.0, -0.5, -1.0, -1.5, -2.0, -3.0, -4.0, -6.0])


def pack_weight(w, fmt):
    k, n = w.shape
    w = f64(bf(w)).reshape(k // 32, 32, n)
    amax = np.abs(w).max(1)
    if fmt == "e4m3":
        byte = np.frexp(amax)[1] - 1 + 127 - 7
    else:
        mant, ex = np.frexp(amax / 6.0)
        byte = np.where(mant > 0.5, ex, ex - 1) + 127
    byte = np.clip(np.where(amax > 0, byte, 1), 1, 254)
    scaled = (w * np.exp2(127.0 - byte)[:, None, :]).reshape(k, n).astype(np.float32)
    by_word = np.ascontiguousarray(scaled.reshape(k // 512, 128, 4, n).transpose(0, 1, 3, 2))
    if fmt == "e4m3":
        words = by_word.astype(ml_dtypes.float8_e4m3fn).view(np.uint8)
    else:
        c = by_word.astype(ml_dtypes.float4_e2m1fn).view(np.uint8) & 0xF
        words = c[..., 0::2] | (c[..., 1::2] << 4)
    return np.ascontiguousarray(words), np.ascontiguousarray(byte.astype(np.uint8).reshape(k // 512, 16, n))


def unpack_weight(words, scales, fmt):
    g, p, n, _ = words.shape
    if fmt == "e4m3":
        vals = np.ascontiguousarray(words).view(ml_dtypes.float8_e4m3fn).astype(np.float64)
    else:
        nib = np.empty((g, p, n, 4), np.uint8)
        nib[..., 0::2] = words & 0xF
        nib[..., 1::2] = words >> 4
        vals = E2M1[nib]
    vals = vals * np.repeat(np.exp2(scales.astype(np.float64) - 127.0), 8, axis=1)[..., None]
    return vals.transpose(0, 1, 3, 2).reshape(g * 512, n)

def pack4(w):
    words, scales = pack_weight(w, "e2m1")
    return words.reshape(words.shape[0], 128, -1), scales


def unpack4(words, scales):
    return unpack_weight(words.reshape(words.shape[0], 128, -1, 2), scales, "e2m1")


B, I, H = 512, 512, 2048
K = I + H


def setup_inputs():
    s = mx_kscale(I)
    sk = np.concatenate([s, np.ones(H)])
    x = bf(np.random.standard_normal((B, I)) * s)
    h = bf(np.random.standard_normal((B, H)))
    time_delta = bf(np.random.uniform(0.0, 1.0, (B, 1)))
    W_mod_words, W_mod_scales = pack4(np.random.standard_normal((K, H)) * 0.6 / np.sqrt(K) / sk[:, None])
    b_mod = bf(np.random.standard_normal(H) * 0.2)
    W_tgt_words, W_tgt_scales = pack4(np.random.standard_normal((K, H)) * 0.6 / np.sqrt(K) / sk[:, None])
    b_tgt = bf(np.random.standard_normal(H) * 0.2)
    log_tau = bf(np.random.standard_normal(H) * 0.2)
    bias = bf(np.random.standard_normal(H) * 0.1)
    return {"x": x,
            "h": h,
            "time_delta": time_delta,
            "W_mod_words": W_mod_words,
            "W_mod_scales": W_mod_scales,
            "b_mod": b_mod,
            "W_tgt_words": W_tgt_words,
            "W_tgt_scales": W_tgt_scales,
            "b_tgt": b_tgt,
            "log_tau": log_tau,
            "bias": bias}


def reference(x, h, time_delta, W_mod_words, W_mod_scales, b_mod, W_tgt_words, W_tgt_scales, b_tgt, log_tau, bias):
    hf = f64(h)
    combined = np.concatenate([f64(x), hf], axis=-1)
    cq = mxq(combined, 1, "e4m3")
    f = np.tanh((cq @ unpack4(W_mod_words, W_mod_scales)) + f64(b_mod))
    a = np.tanh((cq @ unpack4(W_tgt_words, W_tgt_scales)) + f64(b_tgt))
    tau = np.exp(f64(log_tau))[None, :]
    tau_sys = tau / (1.0 + tau * np.abs(f))
    decay = np.exp(-f64(time_delta) / (tau_sys + 1e-6))
    h_new = decay * hf + (1.0 - decay) * (a + f64(bias))
    return h_new

@@ -1,0 +1,315 @@
+from contextlib import ExitStack
+
+import concourse.mybir as mybir
+from concourse.masks import make_identity
+
+F32 = mybir.dt.float32
+BF16 = mybir.dt.bfloat16
+I32 = mybir.dt.int32
+U32 = mybir.dt.uint32
+U8 = mybir.dt.uint8
+FP8X4 = mybir.dt.float8_e4m3fn_x4
+FP4X4 = mybir.dt.float4_e2m1fn_x4
+ACT = mybir.ActivationFunctionType
+ALU = mybir.AluOpType
+
+P = 128
+B, I, H = 512, 512, 2048
+K = I + H
+G = K // 512
+NBT = B // P
+NU = H // P
+NR = NU // 2
+EPS = 1e-6
+
+FLOPS = 2 * 2 * B * K * H
+
+
+def tile_ltccell_kernel(
+    tc, x, h, time_delta, W_mod_words, W_mod_scales, b_mod, W_tgt_words, W_tgt_scales, b_tgt, log_tau, bias, out
+):
+    nc = tc.nc
+    with ExitStack() as ctx:
+        ctx.enter_context(tc.manual_schedule())
+        keep = ctx.enter_context(tc.tile_pool(name="keep", bufs=1))
+        stage = ctx.enter_context(tc.tile_pool(name="stage", bufs=2))
+        work = ctx.enter_context(tc.tile_pool(name="work", bufs=2))
+        psum = ctx.enter_context(tc.psum_pool(name="psum", bufs=4))
+
+        c_sb = keep.tile([P, NBT, K], BF16, name="c_sb", align_bytes=64)
+        w_sb = [keep.tile([P, G, 2 * H], U8, name="w_sb%d" % m, align_bytes=64) for m in range(2)]
+        pl_a = [keep.tile([P, G, 512], U8, name="pl_a%d" % m, align_bytes=64) for m in range(2)]
+        pl_b = [keep.tile([P, G, H - 512], U8, name="pl_b%d" % m, align_bytes=64) for m in range(2)]
+        codes = keep.tile([P, G, B], U32, name="codes", align_bytes=64)
+        cpl = keep.tile([P, G, B], U8, name="cpl", align_bytes=64)
+        ident = keep.tile([P, P], F32, name="ident")
+        crow = keep.tile([P, P], BF16, name="crow")
+        crow32 = keep.tile([P, P], F32, name="crow32")
+        cst = keep.tile([P, P], F32, name="cst")
+        ltc = keep.tile([P, NU], F32, name="ltc")
+        itau = keep.tile([P, NU], F32, name="itau")
+        c1 = keep.tile([P, NU], F32, name="c1")
+        arec = keep.tile([P, NU], F32, name="arec")
+        nbk = keep.tile([P, NU], F32, name="nbk")
+        ntd = keep.tile([P, NBT], F32, name="ntd")
+        warm_in = keep.tile([P, 1], F32, name="warm_in")
+        warm_out = keep.tile([P, 1], F32, name="warm_out")
+
+        words = [W_mod_words, W_tgt_words]
+        scales = [W_mod_scales, W_tgt_scales]
+        w_src = [w.bitcast(I32).rearrange("g p w -> p g w") for w in words]
+        s_src = [s.bitcast(I32).rearrange("g q n -> q g n") for s in scales]
+        h_src = h.rearrange("(t p) k -> p t k", p=P)
+        out_dst = out.rearrange("(t p) n -> p t n", p=P)
+
+        def load_words(m, blk, g_lo=0, g_hi=G):
+            lo, hi = 256 * blk, 256 * (blk + 1)
+            nc.sync.dma_start(
+                out=w_sb[m][:].bitcast(I32)[:, g_lo:g_hi, lo:hi], in_=w_src[m][:, g_lo:g_hi, lo:hi]
+            )
+
+        def load_scales(m, first):
+            plane = pl_a[m] if first else pl_b[m]
+            lo, hi = (0, 128) if first else (128, 512)
+            for r in range(4):
+                nc.sync.dma_start(out=plane[:].bitcast(I32)[r:P:32, :, :], in_=s_src[m][r:16:4, :, lo:hi])
+
+        def load_h(g):
+            nc.sync.dma_start(out=c_sb[:, :, 512 * g : 512 * (g + 1)], in_=h_src[:, :, 512 * (g - 1) : 512 * g])
+
+        nc.vector.memset(warm_in[:], 0.0)
+        nc.scalar.activation(out=warm_out[:], in_=warm_in[:], func=ACT.Tanh)
+        nc.vector.memset(pl_a[0][:].bitcast(I32), 0)
+        nc.vector.memset(crow[:], 0.0)
+        nc.vector.memset(pl_a[1][:].bitcast(I32), 0)
+        nc.vector.memset(pl_b[0][:].bitcast(I32), 0)
+        nc.vector.memset(pl_b[1][:].bitcast(I32), 0)
+        make_identity(nc, ident[:])
+
+        nc.sync.dma_start(out=c_sb[:, :, 0:I], in_=x.rearrange("(t p) k -> p t k", p=P))
+        load_h(1)
+        load_scales(0, True)
+        load_words(0, 0, 0, 1)
+        load_words(0, 0, 1, G)
+        load_h(2)
+        load_h(3)
+        load_h(4)
+        for i, vec in enumerate([b_mod, b_tgt, log_tau, bias]):
+            nc.sync.dma_start(out=crow[NU * i : NU * (i + 1), :], in_=vec.rearrange("(j p) -> j p", p=P))
+        nc.sync.dma_start(out=crow[4 * NU : 4 * NU + NBT, :], in_=time_delta.rearrange("(t p) o -> t (p o)", p=P))
+        load_scales(1, True)
+        load_words(1, 0)
+        load_scales(0, False)
+        load_words(0, 1)
+        load_scales(1, False)
+        load_words(1, 1)
+        for blk in range(2, 4):
+            load_words(0, blk)
+            load_words(1, blk)
+
+        bm = cst[:, 0:NU]
+        bt_ = cst[:, NU : 2 * NU]
+        bias_c = cst[:, 3 * NU : 4 * NU]
+
+        def c_pass(g):
+            grp = stage.tile([P, 4 * B], BF16, name="grp", tag="grp", align_bytes=64)
+            grp32 = grp[:].bitcast(F32).rearrange("p (b u) -> p b u", u=2)
+            for half in range(2):
+                ct = psum.tile([P, 2, 256], F32, name="ct", tag="t")
+                for t2 in range(2):
+                    cw = c_sb[:, 2 * half + t2, :].bitcast(F32)
+                    for u in range(2):
+                        nc.tensor.transpose(
+                            out=ct[:, u, P * t2 : P * (t2 + 1)],
+                            in_=cw[:, 256 * g + u : 256 * (g + 1) : 2],
+                            identity=ident[:],
+                        )
+                dst = grp32[:, 256 * half : 256 * (half + 1), :]
+                src = ct[:].rearrange("p u b -> p b u")
+                if half == 0:
+                    nc.scalar.copy(out=dst, in_=src)
+                else:
+                    nc.vector.tensor_copy(out=dst, in_=src)
+            nc.vector.quantize_mx(out=codes[:, g, :].bitcast(FP8X4), scales=cpl[:, g, :], in_=grp[:])
+
+        def mx_pass(acc, m, j, g):
+            if j < 4:
+                plane = pl_a[m][:, g, P * j : P * (j + 1)]
+            else:
+                plane = pl_b[m][:, g, P * (j - 4) : P * (j - 3)]
+            nc.tensor.matmul_mx(
+                out=acc[:],
+                lhsT=w_sb[m][:, g, 2 * P * j : 2 * P * (j + 1)].bitcast(FP4X4),
+                lhsT_scale=plane,
+                rhs=codes[:, g, :].bitcast(FP8X4),
+                rhs_scale=cpl[:, g, :],
+                start=(g == 0),
+                stop=(g == G - 1),
+            )
+
+        def new_acc():
+            acc = psum.tile([P, B], F32, name="acc", tag="mx")
+            return acc
+
+        def group(m, j):
+            acc = new_acc()
+            for g in range(G):
+                mx_pass(acc, m, j, g)
+            return acc
+
+        def f_chain(acc, j):
+            f = work.tile([P, B], F32, name="f", tag="f", bufs=2)
+            nc.scalar.activation(out=f[:], in_=acc[:], func=ACT.Tanh, bias=bm[:, j : j + 1], scale=1.0)
+            y = work.tile([P, B], F32, name="y", tag="y", bufs=3)
+            nc.scalar.activation(out=y[:], in_=f[:], func=ACT.Abs)
+            t = work.tile([P, B], F32, name="t", tag="t", bufs=2)
+            nc.vector.tensor_scalar(
+                out=t[:], in0=y[:], scalar1=nbk[:, j : j + 1], scalar2=arec[:, j : j + 1], op0=ALU.mult, op1=ALU.add
+            )
+            q = work.tile([P, B], F32, name="q", tag="q", bufs=5)
+            nc.vector.scalar_tensor_tensor(
+                out=q[:], in0=y[:], scalar=itau[:, j : j + 1], in1=t[:], op0=ALU.add, op1=ALU.mult
+            )
+            return q
+
+        def a_tanh(acc, j):
+            a = work.tile([P, B], F32, name="a", tag="a", bufs=3)
+            nc.scalar.activation(out=a[:], in_=acc[:], func=ACT.Tanh, bias=bt_[:, j : j + 1], scale=1.0)
+            return a
+
+        def a_bias(a, j):
+            gt = work.tile([P, B], F32, name="gt", tag="gt", bufs=5)
+            nc.vector.tensor_scalar_add(out=gt[:], in0=a[:], scalar1=bias_c[:, j : j + 1])
+            return gt
+
+        def turn_back(tiles, tag):
+            n = len(tiles)
+            per_bank = 4 // n
+            banks = []
+            for b0 in range(0, NBT, per_bank):
+                bank = psum.tile([P, per_bank, n * P], F32, name="bank", tag=tag)
+                for t2 in range(per_bank):
+                    for k in range(n):
+                        nc.tensor.transpose(
+                            out=bank[:, t2, P * k : P * (k + 1)],
+                            in_=tiles[k][:, P * (b0 + t2) : P * (b0 + t2 + 1)],
+                            identity=ident[:],
+                        )
+                banks.append(bank)
+            return banks
+
+        def decay(banks):
+            dec = work.tile([P, NBT, 2 * P], F32, name="dec", tag="dec", bufs=2)
+            for bt in range(NBT):
+                nc.scalar.activation(
+                    out=dec[:, bt, :], in_=banks[bt // 2][:, bt % 2, :], func=ACT.Exp, scale=ntd[:, bt : bt + 1]
+                )
+            return dec
+
+        def blend_m(lo, width, banks):
+            mt = work.tile([P, NBT, width], F32, name="mt%d" % width, tag="mt%d" % width, bufs=2)
+            per_bank = NBT // len(banks)
+            for i, bank in enumerate(banks):
+                nc.vector.tensor_tensor(
+                    out=mt[:, per_bank * i : per_bank * (i + 1), :],
+                    in0=c_sb[:, per_bank * i : per_bank * (i + 1), I + lo : I + lo + width],
+                    in1=bank[:],
+                    op=ALU.subtract,
+                )
+            return mt
+
+        def blend_eo(lo, width, mt, dec_view):
+            ot = work.tile([P, NBT, width], F32, name="ot%d" % width, tag="ot%d" % width, bufs=3)
+            nc.vector.scalar_tensor_tensor(
+                out=mt[:], in0=dec_view, scalar=1.0, in1=mt[:], op0=ALU.subtract, op1=ALU.mult
+            )
+            nc.vector.tensor_tensor(out=ot[:], in0=c_sb[:, :, I + lo : I + lo + width], in1=mt[:], op=ALU.add)
+            nc.sync.dma_start(out=out_dst[:, :, lo : lo + width], in_=ot[:])
+
+        c_pass(0)
+        c_pass(1)
+        accs = [new_acc() for k in range(4)]
+        for k in range(4):
+            mx_pass(accs[k], 0, k, 0)
+        c_pass(2)
+        for k in range(4):
+            mx_pass(accs[k], 0, k, 1)
+        c_pass(3)
+        for k in range(4):
+            mx_pass(accs[k], 0, k, 2)
+        nc.vector.tensor_copy(out=crow32[:], in_=crow[:])
+        c_pass(4)
+        cps = psum.tile([P, 512], F32, name="cps", tag="t")
+        nc.tensor.transpose(out=cps[:, 0:P], in_=crow32[:], identity=ident[:])
+        nc.vector.tensor_copy(out=cst[:], in_=cps[:, 0:P])
+        nc.vector.tensor_scalar_max(out=ltc[:], in0=cst[:, 2 * NU : 3 * NU], scalar1=-60.0)
+        nc.scalar.activation(out=itau[:], in_=ltc[:], func=ACT.Exp, scale=-1.0)
+        nc.vector.tensor_scalar(out=c1[:], in0=itau[:], scalar1=EPS, scalar2=1.0, op0=ALU.mult, op1=ALU.add)
+        nc.vector.reciprocal(out=arec[:], in_=c1[:])
+        nc.vector.scalar_tensor_tensor(
+            out=nbk[:], in0=arec[:], scalar=-EPS, in1=arec[:], op0=ALU.mult, op1=ALU.mult
+        )
+        nc.vector.tensor_scalar_mul(out=ntd[:], in0=cst[:, 4 * NU : 4 * NU + NBT], scalar1=-1.0)
+        for k in range(4):
+            mx_pass(accs[k], 0, k, 3)
+        for k in range(4):
+            mx_pass(accs[k], 0, k, 4)
+
+        qs = {}
+        gts = {}
+        for k in range(4):
+            qs[k] = f_chain(accs[k], k)
+
+        def a_phase(i):
+            pair = [group(1, 2 * i), group(1, 2 * i + 1)]
+            for k in range(2):
+                gts[2 * i + k] = a_bias(a_tanh(pair[k], 2 * i + k), 2 * i + k)
+
+        def turn_round(i):
+            q_banks = turn_back([qs[2 * i], qs[2 * i + 1]], "t")
+            g_banks = turn_back([gts[2 * i], gts[2 * i + 1]], "t")
+            return q_banks, g_banks
+
+        def finish_round(i, q_banks, g_banks):
+            dec = decay(q_banks)
+            mt = blend_m(2 * P * i, 2 * P, g_banks)
+            blend_eo(2 * P * i, 2 * P, mt, dec[:])
+
+        a_phase(0)
+        a_phase(1)
+        q_banks, g_banks = turn_round(0)
+        finish_round(0, q_banks, g_banks)
+        for i in range(2, NR):
+            pair = [group(0, 2 * i), group(0, 2 * i + 1)]
+            q_banks, g_banks = turn_round(i - 1)
+            for k in range(2):
+                qs[2 * i + k] = f_chain(pair[k], 2 * i + k)
+            if i < NR - 1:
+                finish_round(i - 1, q_banks, g_banks)
+                a_phase(i)
+
+        last = NR - 1
+        u0, u1 = 2 * last, 2 * last + 1
+        dec6 = decay(q_banks)
+        mt6 = blend_m(2 * P * (last - 1), 2 * P, g_banks)
+        acc0 = group(1, u0)
+        a0 = a_tanh(acc0, u0)
+        q_banks = turn_back([qs[u0], qs[u1]], "mx")
+        dec7 = decay(q_banks)
+        acc1 = group(1, u1)
+        a1 = a_tanh(acc1, u1)
+        nc.vector.scalar_tensor_tensor(
+            out=mt6[:], in0=dec6[:], scalar=1.0, in1=mt6[:], op0=ALU.subtract, op1=ALU.mult
+        )
+        g0 = a_bias(a0, u0)
+        ot6 = work.tile([P, NBT, 2 * P], F32, name="ot256", tag="ot256", bufs=3)
+        lo6 = 2 * P * (last - 1)
+        nc.vector.tensor_tensor(out=ot6[:], in0=c_sb[:, :, I + lo6 : I + lo6 + 2 * P], in1=mt6[:], op=ALU.add)
+        nc.sync.dma_start(out=out_dst[:, :, lo6 : lo6 + 2 * P], in_=ot6[:])
+        g1 = a_bias(a1, u1)
+        bank0 = turn_back([g0], "t")
+        bank1 = turn_back([g1], "t")
+        m0 = blend_m(P * u0, P, bank0)
+        blend_eo(P * u0, P, m0, dec7[:, :, 0:P])
+        m1 = blend_m(P * u1, P, bank1)
+        blend_eo(P * u1, P, m1, dec7[:, :, P : 2 * P])

@@ -126,10 +126,7 @@ def tile_ltccell_kernel(
                         )
                 dst = grp32[:, 256 * half : 256 * (half + 1), :]
                 src = ct[:].rearrange("p u b -> p b u")
-                if half == 0:
-                    nc.scalar.copy(out=dst, in_=src)
-                else:
-                    nc.vector.tensor_copy(out=dst, in_=src)
+                nc.scalar.copy(out=dst, in_=src)
             nc.vector.quantize_mx(out=codes[:, g, :].bitcast(FP8X4), scales=cpl[:, g, :], in_=grp[:])
 
         def mx_pass(acc, m, j, g):
@@ -157,15 +154,24 @@ def tile_ltccell_kernel(
                 mx_pass(acc, m, j, g)
             return acc
 
-        def f_chain(acc, j):
-            f = work.tile([P, B], F32, name="f", tag="f", bufs=2)
+        def f_tanh(acc, j):
+            f = work.tile([P, B], F32, name="f", tag="f", bufs=4)
             nc.scalar.activation(out=f[:], in_=acc[:], func=ACT.Tanh, bias=bm[:, j : j + 1], scale=1.0)
-            y = work.tile([P, B], F32, name="y", tag="y", bufs=3)
+            return f
+
+        def f_abs(f):
+            y = work.tile([P, B], F32, name="y", tag="y", bufs=4)
             nc.scalar.activation(out=y[:], in_=f[:], func=ACT.Abs)
-            t = work.tile([P, B], F32, name="t", tag="t", bufs=2)
+            return y
+
+        def f_lin(y, j):
+            t = work.tile([P, B], F32, name="t", tag="t", bufs=4)
             nc.vector.tensor_scalar(
                 out=t[:], in0=y[:], scalar1=nbk[:, j : j + 1], scalar2=arec[:, j : j + 1], op0=ALU.mult, op1=ALU.add
             )
+            return t
+
+        def f_rate(y, t, j):
             q = work.tile([P, B], F32, name="q", tag="q", bufs=5)
             nc.vector.scalar_tensor_tensor(
                 out=q[:], in0=y[:], scalar=itau[:, j : j + 1], in1=t[:], op0=ALU.add, op1=ALU.mult
@@ -173,7 +179,7 @@ def tile_ltccell_kernel(
             return q
 
         def a_tanh(acc, j):
-            a = work.tile([P, B], F32, name="a", tag="a", bufs=3)
+            a = work.tile([P, B], F32, name="a", tag="a", bufs=4)
             nc.scalar.activation(out=a[:], in_=acc[:], func=ACT.Tanh, bias=bt_[:, j : j + 1], scale=1.0)
             return a
 
@@ -206,24 +212,32 @@ def tile_ltccell_kernel(
                 )
             return dec
 
-        def blend_m(lo, width, banks):
-            mt = work.tile([P, NBT, width], F32, name="mt%d" % width, tag="mt%d" % width, bufs=2)
-            per_bank = NBT // len(banks)
-            for i, bank in enumerate(banks):
-                nc.vector.tensor_tensor(
-                    out=mt[:, per_bank * i : per_bank * (i + 1), :],
-                    in0=c_sb[:, per_bank * i : per_bank * (i + 1), I + lo : I + lo + width],
-                    in1=bank[:],
-                    op=ALU.subtract,
-                )
-            return mt
-
-        def blend_eo(lo, width, mt, dec_view):
-            ot = work.tile([P, NBT, width], F32, name="ot%d" % width, tag="ot%d" % width, bufs=3)
-            nc.vector.scalar_tensor_tensor(
-                out=mt[:], in0=dec_view, scalar=1.0, in1=mt[:], op0=ALU.subtract, op1=ALU.mult
+        def b_sub(mt, lo, width, t_lo, t_hi, bank):
+            nc.vector.tensor_tensor(
+                out=mt[:, t_lo:t_hi, :], in0=c_sb[:, t_lo:t_hi, I + lo : I + lo + width], in1=bank[:], op=ALU.subtract
             )
-            nc.vector.tensor_tensor(out=ot[:], in0=c_sb[:, :, I + lo : I + lo + width], in1=mt[:], op=ALU.add)
+
+        def b_mul(mt, dec_view, t_lo, t_hi):
+            nc.vector.scalar_tensor_tensor(
+                out=mt[:, t_lo:t_hi, :],
+                in0=dec_view[:, t_lo:t_hi, :],
+                scalar=1.0,
+                in1=mt[:, t_lo:t_hi, :],
+                op0=ALU.subtract,
+                op1=ALU.mult,
+            )
+
+        def b_add(ot, mt, lo, width, t_lo, t_hi):
+            nc.vector.tensor_tensor(
+                out=ot[:, t_lo:t_hi, :], in0=c_sb[:, t_lo:t_hi, I + lo : I + lo + width], in1=mt[:, t_lo:t_hi, :], op=ALU.add
+            )
+
+        def b_tiles(width):
+            mt = work.tile([P, NBT, width], F32, name="mt%d" % width, tag="mt%d" % width, bufs=2)
+            ot = work.tile([P, NBT, width], F32, name="ot%d" % width, tag="ot%d" % width, bufs=3)
+            return mt, ot
+
+        def store(ot, lo, width):
             nc.sync.dma_start(out=out_dst[:, :, lo : lo + width], in_=ot[:])
 
         c_pass(0)
@@ -255,61 +269,54 @@ def tile_ltccell_kernel(
         for k in range(4):
             mx_pass(accs[k], 0, k, 4)
 
+        W2 = 2 * P
         qs = {}
         gts = {}
+        fs = [f_tanh(accs[k], k) for k in range(4)]
+        ys = [f_abs(fs[k]) for k in range(4)]
+        acc_a = [group(1, 0), group(1, 1), group(1, 2), group(1, 3)]
+        ts = [f_lin(ys[k], k) for k in range(4)]
         for k in range(4):
-            qs[k] = f_chain(accs[k], k)
+            qs[k] = f_rate(ys[k], ts[k], k)
+        a_s = [a_tanh(acc_a[k], k) for k in range(4)]
+        for k in range(4):
+            gts[k] = a_bias(a_s[k], k)
 
-        def a_phase(i):
-            pair = [group(1, 2 * i), group(1, 2 * i + 1)]
-            for k in range(2):
-                gts[2 * i + k] = a_bias(a_tanh(pair[k], 2 * i + k), 2 * i + k)
-
-        def turn_round(i):
-            q_banks = turn_back([qs[2 * i], qs[2 * i + 1]], "t")
-            g_banks = turn_back([gts[2 * i], gts[2 * i + 1]], "t")
-            return q_banks, g_banks
-
-        def finish_round(i, q_banks, g_banks):
+        for i in range(1, NR + 1):
+            ua, ub = 2 * i, 2 * i + 1
+            new = 2 <= i < NR
+            if new:
+                acc_f = [group(0, ua), group(0, ub)]
+            lo = W2 * (i - 1)
+            q_banks = turn_back([qs[ua - 2], qs[ub - 2]], "t")
+            g_banks = turn_back([gts[ua - 2], gts[ub - 2]], "t")
+            if new:
+                fa = f_tanh(acc_f[0], ua)
+                ya = f_abs(fa)
+                fb = f_tanh(acc_f[1], ub)
+                yb = f_abs(fb)
             dec = decay(q_banks)
-            mt = blend_m(2 * P * i, 2 * P, g_banks)
-            blend_eo(2 * P * i, 2 * P, mt, dec[:])
-
-        a_phase(0)
-        a_phase(1)
-        q_banks, g_banks = turn_round(0)
-        finish_round(0, q_banks, g_banks)
-        for i in range(2, NR):
-            pair = [group(0, 2 * i), group(0, 2 * i + 1)]
-            q_banks, g_banks = turn_round(i - 1)
-            for k in range(2):
-                qs[2 * i + k] = f_chain(pair[k], 2 * i + k)
-            if i < NR - 1:
-                finish_round(i - 1, q_banks, g_banks)
-                a_phase(i)
-
-        last = NR - 1
-        u0, u1 = 2 * last, 2 * last + 1
-        dec6 = decay(q_banks)
-        mt6 = blend_m(2 * P * (last - 1), 2 * P, g_banks)
-        acc0 = group(1, u0)
-        a0 = a_tanh(acc0, u0)
-        q_banks = turn_back([qs[u0], qs[u1]], "mx")
-        dec7 = decay(q_banks)
-        acc1 = group(1, u1)
-        a1 = a_tanh(acc1, u1)
-        nc.vector.scalar_tensor_tensor(
-            out=mt6[:], in0=dec6[:], scalar=1.0, in1=mt6[:], op0=ALU.subtract, op1=ALU.mult
-        )
-        g0 = a_bias(a0, u0)
-        ot6 = work.tile([P, NBT, 2 * P], F32, name="ot256", tag="ot256", bufs=3)
-        lo6 = 2 * P * (last - 1)
-        nc.vector.tensor_tensor(out=ot6[:], in0=c_sb[:, :, I + lo6 : I + lo6 + 2 * P], in1=mt6[:], op=ALU.add)
-        nc.sync.dma_start(out=out_dst[:, :, lo6 : lo6 + 2 * P], in_=ot6[:])
-        g1 = a_bias(a1, u1)
-        bank0 = turn_back([g0], "t")
-        bank1 = turn_back([g1], "t")
-        m0 = blend_m(P * u0, P, bank0)
-        blend_eo(P * u0, P, m0, dec7[:, :, 0:P])
-        m1 = blend_m(P * u1, P, bank1)
-        blend_eo(P * u1, P, m1, dec7[:, :, P : 2 * P])
+            if new:
+                acc_a = [group(1, ua), group(1, ub)]
+                aa = a_tanh(acc_a[0], ua)
+                ab = a_tanh(acc_a[1], ub)
+            mt, ot = b_tiles(W2)
+            if new:
+                ta = f_lin(ya, ua)
+            b_sub(mt, lo, W2, 0, 2, g_banks[0])
+            if new:
+                tb = f_lin(yb, ub)
+            b_sub(mt, lo, W2, 2, 4, g_banks[1])
+            if new:
+                qs[ua] = f_rate(ya, ta, ua)
+            b_mul(mt, dec, 0, 2)
+            if new:
+                qs[ub] = f_rate(yb, tb, ub)
+            b_mul(mt, dec, 2, 4)
+            b_add(ot, mt, lo, W2, 0, 2)
+            if new:
+                gts[ua] = a_bias(aa, ua)
+            b_add(ot, mt, lo, W2, 2, 4)
+            store(ot, lo, W2)
+            if new:
+                gts[ub] = a_bias(ab, ub)

@@ -205,7 +205,7 @@ def tile_ltccell_kernel(
             return banks
 
         def decay(banks):
-            dec = work.tile([P, NBT, 2 * P], F32, name="dec", tag="dec", bufs=2)
+            dec = work.tile([P, NBT, 2 * P], F32, name="dec", tag="dec", bufs=3)
             for bt in range(NBT):
                 nc.scalar.activation(
                     out=dec[:, bt, :], in_=banks[bt // 2][:, bt % 2, :], func=ACT.Exp, scale=ntd[:, bt : bt + 1]
@@ -272,51 +272,74 @@ def tile_ltccell_kernel(
         W2 = 2 * P
         qs = {}
         gts = {}
+        decs = {}
+
+        def turn_q(i):
+            decs[i] = decay(turn_back([qs[2 * i], qs[2 * i + 1]], "t"))
+
+        def turn_g(i):
+            return turn_back([gts[2 * i], gts[2 * i + 1]], "t")
+
         fs = [f_tanh(accs[k], k) for k in range(4)]
         ys = [f_abs(fs[k]) for k in range(4)]
-        acc_a = [group(1, 0), group(1, 1), group(1, 2), group(1, 3)]
+        acc_a = [group(1, 0), group(1, 1)]
+        a_s = [a_tanh(acc_a[k], k) for k in range(2)]
         ts = [f_lin(ys[k], k) for k in range(4)]
         for k in range(4):
             qs[k] = f_rate(ys[k], ts[k], k)
-        a_s = [a_tanh(acc_a[k], k) for k in range(4)]
-        for k in range(4):
+        for k in range(2):
             gts[k] = a_bias(a_s[k], k)
+        turn_q(0)
+        a2 = a_tanh(group(1, 2), 2)
+        g_banks = turn_g(0)
+        a3 = a_tanh(group(1, 3), 3)
+        mt, ot = b_tiles(W2)
+        b_sub(mt, 0, W2, 0, 2, g_banks[0])
+        b_sub(mt, 0, W2, 2, 4, g_banks[1])
+        gts[2] = a_bias(a2, 2)
+        b_mul(mt, decs[0], 0, 2)
+        b_mul(mt, decs[0], 2, 4)
+        gts[3] = a_bias(a3, 3)
+        b_add(ot, mt, 0, W2, 0, 2)
+        b_add(ot, mt, 0, W2, 2, 4)
+        store(ot, 0, W2)
+        turn_q(1)
 
-        for i in range(1, NR + 1):
+        for i in range(2, NR):
             ua, ub = 2 * i, 2 * i + 1
-            new = 2 <= i < NR
-            if new:
-                acc_f = [group(0, ua), group(0, ub)]
             lo = W2 * (i - 1)
-            q_banks = turn_back([qs[ua - 2], qs[ub - 2]], "t")
-            g_banks = turn_back([gts[ua - 2], gts[ub - 2]], "t")
-            if new:
-                fa = f_tanh(acc_f[0], ua)
-                ya = f_abs(fa)
-                fb = f_tanh(acc_f[1], ub)
-                yb = f_abs(fb)
-            dec = decay(q_banks)
-            if new:
-                acc_a = [group(1, ua), group(1, ub)]
-                aa = a_tanh(acc_a[0], ua)
-                ab = a_tanh(acc_a[1], ub)
+            acc_f = [group(0, ua), group(0, ub)]
+            g_banks = turn_g(i - 1)
+            fa = f_tanh(acc_f[0], ua)
+            ya = f_abs(fa)
+            fb = f_tanh(acc_f[1], ub)
+            yb = f_abs(fb)
+            acc_a = [group(1, ua), group(1, ub)]
+            aa = a_tanh(acc_a[0], ua)
+            ab = a_tanh(acc_a[1], ub)
             mt, ot = b_tiles(W2)
-            if new:
-                ta = f_lin(ya, ua)
+            ta = f_lin(ya, ua)
             b_sub(mt, lo, W2, 0, 2, g_banks[0])
-            if new:
-                tb = f_lin(yb, ub)
+            qs[ua] = f_rate(ya, ta, ua)
+            tb = f_lin(yb, ub)
             b_sub(mt, lo, W2, 2, 4, g_banks[1])
-            if new:
-                qs[ua] = f_rate(ya, ta, ua)
-            b_mul(mt, dec, 0, 2)
-            if new:
-                qs[ub] = f_rate(yb, tb, ub)
-            b_mul(mt, dec, 2, 4)
+            qs[ub] = f_rate(yb, tb, ub)
+            turn_q(i)
+            b_mul(mt, decs[i - 1], 0, 2)
+            b_mul(mt, decs[i - 1], 2, 4)
+            gts[ua] = a_bias(aa, ua)
             b_add(ot, mt, lo, W2, 0, 2)
-            if new:
-                gts[ua] = a_bias(aa, ua)
+            gts[ub] = a_bias(ab, ub)
             b_add(ot, mt, lo, W2, 2, 4)
             store(ot, lo, W2)
-            if new:
-                gts[ub] = a_bias(ab, ub)
+
+        lo = W2 * (NR - 1)
+        g_banks = turn_g(NR - 1)
+        mt, ot = b_tiles(W2)
+        b_sub(mt, lo, W2, 0, 2, g_banks[0])
+        b_sub(mt, lo, W2, 2, 4, g_banks[1])
+        b_mul(mt, decs[NR - 1], 0, 2)
+        b_mul(mt, decs[NR - 1], 2, 4)
+        b_add(ot, mt, lo, W2, 0, 2)
+        b_add(ot, mt, lo, W2, 2, 4)
+        store(ot, lo, W2)

@@ -36,8 +36,11 @@ def tile_ltccell_kernel(
         work = ctx.enter_context(tc.tile_pool(name="work", bufs=2))
         psum = ctx.enter_context(tc.psum_pool(name="psum", bufs=4))
 
-        c_sb = keep.tile([P, NBT, K], BF16, name="c_sb", align_bytes=64)
-        w_sb = [keep.tile([P, G, 2 * H], U8, name="w_sb%d" % m, align_bytes=64) for m in range(2)]
+        c_t = [keep.tile([P, NBT, 512], BF16, name="c_t%d" % g, align_bytes=64) for g in range(G)]
+        w_t = [
+            [keep.tile([P, G, 1024], U8, name="w_t%d_%d" % (m, blk), align_bytes=64) for blk in range(4)]
+            for m in range(2)
+        ]
         pl_a = [keep.tile([P, G, 512], U8, name="pl_a%d" % m, align_bytes=64) for m in range(2)]
         pl_b = [keep.tile([P, G, H - 512], U8, name="pl_b%d" % m, align_bytes=64) for m in range(2)]
         codes = keep.tile([P, G, B], U32, name="codes", align_bytes=64)
@@ -64,9 +67,7 @@ def tile_ltccell_kernel(
 
         def load_words(m, blk, g_lo=0, g_hi=G):
             lo, hi = 256 * blk, 256 * (blk + 1)
-            nc.sync.dma_start(
-                out=w_sb[m][:].bitcast(I32)[:, g_lo:g_hi, lo:hi], in_=w_src[m][:, g_lo:g_hi, lo:hi]
-            )
+            nc.sync.dma_start(out=w_t[m][blk][:].bitcast(I32)[:, g_lo:g_hi, :], in_=w_src[m][:, g_lo:g_hi, lo:hi])
 
         def load_scales(m, first):
             plane = pl_a[m] if first else pl_b[m]
@@ -75,7 +76,7 @@ def tile_ltccell_kernel(
                 nc.sync.dma_start(out=plane[:].bitcast(I32)[r:P:32, :, :], in_=s_src[m][r:16:4, :, lo:hi])
 
         def load_h(g):
-            nc.sync.dma_start(out=c_sb[:, :, 512 * g : 512 * (g + 1)], in_=h_src[:, :, 512 * (g - 1) : 512 * g])
+            nc.sync.dma_start(out=c_t[g][:], in_=h_src[:, :, 512 * (g - 1) : 512 * g])
 
         nc.vector.memset(warm_in[:], 0.0)
         nc.scalar.activation(out=warm_out[:], in_=warm_in[:], func=ACT.Tanh)
@@ -86,7 +87,7 @@ def tile_ltccell_kernel(
         nc.vector.memset(pl_b[1][:].bitcast(I32), 0)
         make_identity(nc, ident[:])
 
-        nc.sync.dma_start(out=c_sb[:, :, 0:I], in_=x.rearrange("(t p) k -> p t k", p=P))
+        nc.sync.dma_start(out=c_t[0][:], in_=x.rearrange("(t p) k -> p t k", p=P))
         load_h(1)
         load_scales(0, True)
         load_words(0, 0, 0, 1)
@@ -117,11 +118,11 @@ def tile_ltccell_kernel(
             for half in range(2):
                 ct = psum.tile([P, 2, 256], F32, name="ct", tag="t")
                 for t2 in range(2):
-                    cw = c_sb[:, 2 * half + t2, :].bitcast(F32)
+                    cw = c_t[g][:, 2 * half + t2, :].bitcast(F32)
                     for u in range(2):
                         nc.tensor.transpose(
                             out=ct[:, u, P * t2 : P * (t2 + 1)],
-                            in_=cw[:, 256 * g + u : 256 * (g + 1) : 2],
+                            in_=cw[:, u:256:2],
                             identity=ident[:],
                         )
                 dst = grp32[:, 256 * half : 256 * (half + 1), :]
@@ -136,7 +137,7 @@ def tile_ltccell_kernel(
                 plane = pl_b[m][:, g, P * (j - 4) : P * (j - 3)]
             nc.tensor.matmul_mx(
                 out=acc[:],
-                lhsT=w_sb[m][:, g, 2 * P * j : 2 * P * (j + 1)].bitcast(FP4X4),
+                lhsT=w_t[m][j // 4][:, g, 2 * P * (j % 4) : 2 * P * (j % 4 + 1)].bitcast(FP4X4),
                 lhsT_scale=plane,
                 rhs=codes[:, g, :].bitcast(FP8X4),
                 rhs_scale=cpl[:, g, :],
@@ -205,16 +206,19 @@ def tile_ltccell_kernel(
             return banks
 
         def decay(banks):
-            dec = work.tile([P, NBT, 2 * P], F32, name="dec", tag="dec", bufs=3)
+            dec = work.tile([P, NBT, 2 * P], F32, name="dec", tag="dec", bufs=2)
             for bt in range(NBT):
                 nc.scalar.activation(
                     out=dec[:, bt, :], in_=banks[bt // 2][:, bt % 2, :], func=ACT.Exp, scale=ntd[:, bt : bt + 1]
                 )
             return dec
 
+        def h_part(lo, width, t_lo, t_hi):
+            return c_t[1 + lo // 512][:, t_lo:t_hi, lo % 512 : lo % 512 + width]
+
         def b_sub(mt, lo, width, t_lo, t_hi, bank):
             nc.vector.tensor_tensor(
-                out=mt[:, t_lo:t_hi, :], in0=c_sb[:, t_lo:t_hi, I + lo : I + lo + width], in1=bank[:], op=ALU.subtract
+                out=mt[:, t_lo:t_hi, :], in0=h_part(lo, width, t_lo, t_hi), in1=bank[:], op=ALU.subtract
             )
 
         def b_mul(mt, dec_view, t_lo, t_hi):
@@ -229,7 +233,7 @@ def tile_ltccell_kernel(
 
         def b_add(ot, mt, lo, width, t_lo, t_hi):
             nc.vector.tensor_tensor(
-                out=ot[:, t_lo:t_hi, :], in0=c_sb[:, t_lo:t_hi, I + lo : I + lo + width], in1=mt[:, t_lo:t_hi, :], op=ALU.add
+                out=ot[:, t_lo:t_hi, :], in0=h_part(lo, width, t_lo, t_hi), in1=mt[:, t_lo:t_hi, :], op=ALU.add
             )
 
         def b_tiles(width):
@@ -272,74 +276,51 @@ def tile_ltccell_kernel(
         W2 = 2 * P
         qs = {}
         gts = {}
-        decs = {}
-
-        def turn_q(i):
-            decs[i] = decay(turn_back([qs[2 * i], qs[2 * i + 1]], "t"))
-
-        def turn_g(i):
-            return turn_back([gts[2 * i], gts[2 * i + 1]], "t")
-
         fs = [f_tanh(accs[k], k) for k in range(4)]
         ys = [f_abs(fs[k]) for k in range(4)]
-        acc_a = [group(1, 0), group(1, 1)]
-        a_s = [a_tanh(acc_a[k], k) for k in range(2)]
+        acc_a = [group(1, 0), group(1, 1), group(1, 2), group(1, 3)]
         ts = [f_lin(ys[k], k) for k in range(4)]
         for k in range(4):
             qs[k] = f_rate(ys[k], ts[k], k)
-        for k in range(2):
+        a_s = [a_tanh(acc_a[k], k) for k in range(4)]
+        for k in range(4):
             gts[k] = a_bias(a_s[k], k)
-        turn_q(0)
-        a2 = a_tanh(group(1, 2), 2)
-        g_banks = turn_g(0)
-        a3 = a_tanh(group(1, 3), 3)
-        mt, ot = b_tiles(W2)
-        b_sub(mt, 0, W2, 0, 2, g_banks[0])
-        b_sub(mt, 0, W2, 2, 4, g_banks[1])
-        gts[2] = a_bias(a2, 2)
-        b_mul(mt, decs[0], 0, 2)
-        b_mul(mt, decs[0], 2, 4)
-        gts[3] = a_bias(a3, 3)
-        b_add(ot, mt, 0, W2, 0, 2)
-        b_add(ot, mt, 0, W2, 2, 4)
-        store(ot, 0, W2)
-        turn_q(1)
 
-        for i in range(2, NR):
+        for i in range(1, NR + 1):
             ua, ub = 2 * i, 2 * i + 1
+            new = 2 <= i < NR
+            if new:
+                acc_f = [group(0, ua), group(0, ub)]
             lo = W2 * (i - 1)
-            acc_f = [group(0, ua), group(0, ub)]
-            g_banks = turn_g(i - 1)
-            fa = f_tanh(acc_f[0], ua)
-            ya = f_abs(fa)
-            fb = f_tanh(acc_f[1], ub)
-            yb = f_abs(fb)
-            acc_a = [group(1, ua), group(1, ub)]
-            aa = a_tanh(acc_a[0], ua)
-            ab = a_tanh(acc_a[1], ub)
+            q_banks = turn_back([qs[ua - 2], qs[ub - 2]], "t")
+            g_banks = turn_back([gts[ua - 2], gts[ub - 2]], "t")
+            if new:
+                fa = f_tanh(acc_f[0], ua)
+                ya = f_abs(fa)
+                fb = f_tanh(acc_f[1], ub)
+                yb = f_abs(fb)
+            dec = decay(q_banks)
+            if new:
+                acc_a = [group(1, ua), group(1, ub)]
+                aa = a_tanh(acc_a[0], ua)
+                ab = a_tanh(acc_a[1], ub)
             mt, ot = b_tiles(W2)
-            ta = f_lin(ya, ua)
+            if new:
+                ta = f_lin(ya, ua)
             b_sub(mt, lo, W2, 0, 2, g_banks[0])
-            qs[ua] = f_rate(ya, ta, ua)
-            tb = f_lin(yb, ub)
+            if new:
+                tb = f_lin(yb, ub)
             b_sub(mt, lo, W2, 2, 4, g_banks[1])
-            qs[ub] = f_rate(yb, tb, ub)
-            turn_q(i)
-            b_mul(mt, decs[i - 1], 0, 2)
-            b_mul(mt, decs[i - 1], 2, 4)
-            gts[ua] = a_bias(aa, ua)
+            if new:
+                qs[ua] = f_rate(ya, ta, ua)
+            b_mul(mt, dec, 0, 2)
+            if new:
+                qs[ub] = f_rate(yb, tb, ub)
+            b_mul(mt, dec, 2, 4)
             b_add(ot, mt, lo, W2, 0, 2)
-            gts[ub] = a_bias(ab, ub)
+            if new:
+                gts[ua] = a_bias(aa, ua)
             b_add(ot, mt, lo, W2, 2, 4)
             store(ot, lo, W2)
-
-        lo = W2 * (NR - 1)
-        g_banks = turn_g(NR - 1)
-        mt, ot = b_tiles(W2)
-        b_sub(mt, lo, W2, 0, 2, g_banks[0])
-        b_sub(mt, lo, W2, 2, 4, g_banks[1])
-        b_mul(mt, decs[NR - 1], 0, 2)
-        b_mul(mt, decs[NR - 1], 2, 4)
-        b_add(ot, mt, lo, W2, 0, 2)
-        b_add(ot, mt, lo, W2, 2, 4)
-        store(ot, lo, W2)
+            if new:
+                gts[ub] = a_bias(ab, ub)

@@ -21,6 +21,8 @@ NBT = B // P
 NU = H // P
 NR = NU // 2
 EPS = 1e-6
+WARM_HEAD = 8
+WARM_GAP = 3
 
 FLOPS = 2 * 2 * B * K * H
 
@@ -36,7 +38,8 @@ def tile_ltccell_kernel(
         work = ctx.enter_context(tc.tile_pool(name="work", bufs=2))
         psum = ctx.enter_context(tc.psum_pool(name="psum", bufs=4))
 
-        c_t = [keep.tile([P, NBT, 512], BF16, name="c_t%d" % g, align_bytes=64) for g in range(G)]
+        x_t = [keep.tile([P, 2, 512], BF16, name="x_t%d" % half, align_bytes=64) for half in range(2)]
+        c_t = [None] + [keep.tile([P, NBT, 512], BF16, name="c_t%d" % g, align_bytes=64) for g in range(1, G)]
         w_t = [
             [keep.tile([P, G, 1024], U8, name="w_t%d_%d" % (m, blk), align_bytes=64) for blk in range(4)]
             for m in range(2)
@@ -57,6 +60,7 @@ def tile_ltccell_kernel(
         ntd = keep.tile([P, NBT], F32, name="ntd")
         warm_in = keep.tile([P, 1], F32, name="warm_in")
         warm_out = keep.tile([P, 1], F32, name="warm_out")
+        zeros = keep.tile([P, 512], BF16, name="zeros")
 
         words = [W_mod_words, W_tgt_words]
         scales = [W_mod_scales, W_tgt_scales]
@@ -78,6 +82,7 @@ def tile_ltccell_kernel(
         def load_h(g):
             nc.sync.dma_start(out=c_t[g][:], in_=h_src[:, :, 512 * (g - 1) : 512 * g])
 
+        nc.vector.memset(zeros[:], 0.0)
         nc.vector.memset(warm_in[:], 0.0)
         nc.scalar.activation(out=warm_out[:], in_=warm_in[:], func=ACT.Tanh)
         nc.vector.memset(pl_a[0][:].bitcast(I32), 0)
@@ -87,7 +92,9 @@ def tile_ltccell_kernel(
         nc.vector.memset(pl_b[1][:].bitcast(I32), 0)
         make_identity(nc, ident[:])
 
-        nc.sync.dma_start(out=c_t[0][:], in_=x.rearrange("(t p) k -> p t k", p=P))
+        x_src = x.rearrange("(t p) k -> p t k", p=P)
+        for half in range(2):
+            nc.sync.dma_start(out=x_t[half][:], in_=x_src[:, 2 * half : 2 * half + 2, :])
         load_h(1)
         load_scales(0, True)
         load_words(0, 0, 0, 1)
@@ -118,7 +125,8 @@ def tile_ltccell_kernel(
             for half in range(2):
                 ct = psum.tile([P, 2, 256], F32, name="ct", tag="t")
                 for t2 in range(2):
-                    cw = c_t[g][:, 2 * half + t2, :].bitcast(F32)
+                    rows = x_t[half][:, t2, :] if g == 0 else c_t[g][:, 2 * half + t2, :]
+                    cw = rows.bitcast(F32)
                     for u in range(2):
                         nc.tensor.transpose(
                             out=ct[:, u, P * t2 : P * (t2 + 1)],
@@ -244,8 +252,16 @@ def tile_ltccell_kernel(
         def store(ot, lo, width):
             nc.sync.dma_start(out=out_dst[:, :, lo : lo + width], in_=ot[:])
 
+        def idle_passes(n):
+            for k in range(n):
+                nc.tensor.matmul(out=spare[:], lhsT=zeros[:, 0:P], rhs=zeros[:], start=True, stop=True)
+
+        spare = new_acc()
+        idle_passes(WARM_HEAD)
         c_pass(0)
+        idle_passes(WARM_GAP)
         c_pass(1)
+        idle_passes(WARM_GAP)
         accs = [new_acc() for k in range(4)]
         for k in range(4):
             mx_pass(accs[k], 0, k, 0)
@@ -286,9 +302,9 @@ def tile_ltccell_kernel(
         for k in range(4):
             gts[k] = a_bias(a_s[k], k)
 
-        for i in range(1, NR + 1):
+        for i in range(1, NR):
             ua, ub = 2 * i, 2 * i + 1
-            new = 2 <= i < NR
+            new = i >= 2
             if new:
                 acc_f = [group(0, ua), group(0, ub)]
             lo = W2 * (i - 1)
@@ -317,10 +333,26 @@ def tile_ltccell_kernel(
             if new:
                 qs[ub] = f_rate(yb, tb, ub)
             b_mul(mt, dec, 2, 4)
-            b_add(ot, mt, lo, W2, 0, 2)
             if new:
                 gts[ua] = a_bias(aa, ua)
-            b_add(ot, mt, lo, W2, 2, 4)
-            store(ot, lo, W2)
+            b_add(ot, mt, lo, W2, 0, 2)
             if new:
                 gts[ub] = a_bias(ab, ub)
+            b_add(ot, mt, lo, W2, 2, 4)
+            store(ot, lo, W2)
+
+        ua, ub = NU - 2, NU - 1
+        q_banks = turn_back([qs[ua], qs[ub]], "t")
+        bank_a = turn_back([gts[ua]], "t")
+        bank_b = turn_back([gts[ub]], "t")
+        dec = decay(q_banks)
+        mt_a, ot_a = b_tiles(P)
+        mt_b, ot_b = b_tiles(P)
+        b_sub(mt_a, P * ua, P, 0, 4, bank_a[0])
+        b_sub(mt_b, P * ub, P, 0, 4, bank_b[0])
+        b_mul(mt_a, dec[:, :, 0:P], 0, 4)
+        b_mul(mt_b, dec[:, :, P:W2], 0, 4)
+        b_add(ot_a, mt_a, P * ua, P, 0, 4)
+        store(ot_a, P * ua, P)
+        b_add(ot_b, mt_b, P * ub, P, 0, 4)
+        store(ot_b, P * ub, P)

@@ -98,8 +98,8 @@ def tile_ltccell_kernel(
         load_h(1)
         load_scales(0, True)
         load_words(0, 0, 0, 1)
-        load_words(0, 0, 1, G)
         load_h(2)
+        load_words(0, 0, 1, G)
         load_h(3)
         load_h(4)
         for i, vec in enumerate([b_mod, b_tgt, log_tau, bias]):
@@ -135,7 +135,10 @@ def tile_ltccell_kernel(
                         )
                 dst = grp32[:, 256 * half : 256 * (half + 1), :]
                 src = ct[:].rearrange("p u b -> p b u")
-                nc.scalar.copy(out=dst, in_=src)
+                if half == 0:
+                    nc.scalar.copy(out=dst, in_=src)
+                else:
+                    nc.vector.tensor_copy(out=dst, in_=src)
             nc.vector.quantize_mx(out=codes[:, g, :].bitcast(FP8X4), scales=cpl[:, g, :], in_=grp[:])
 
         def mx_pass(acc, m, j, g):
@@ -261,7 +264,6 @@ def tile_ltccell_kernel(
         c_pass(0)
         idle_passes(WARM_GAP)
         c_pass(1)
-        idle_passes(WARM_GAP)
         accs = [new_acc() for k in range(4)]
         for k in range(4):
             mx_pass(accs[k], 0, k, 0)
@@ -269,8 +271,6 @@ def tile_ltccell_kernel(
         for k in range(4):
             mx_pass(accs[k], 0, k, 1)
         c_pass(3)
-        for k in range(4):
-            mx_pass(accs[k], 0, k, 2)
         nc.vector.tensor_copy(out=crow32[:], in_=crow[:])
         c_pass(4)
         cps = psum.tile([P, 512], F32, name="cps", tag="t")
@@ -284,10 +284,9 @@ def tile_ltccell_kernel(
             out=nbk[:], in0=arec[:], scalar=-EPS, in1=arec[:], op0=ALU.mult, op1=ALU.mult
         )
         nc.vector.tensor_scalar_mul(out=ntd[:], in0=cst[:, 4 * NU : 4 * NU + NBT], scalar1=-1.0)
-        for k in range(4):
-            mx_pass(accs[k], 0, k, 3)
-        for k in range(4):
-            mx_pass(accs[k], 0, k, 4)
+        for g in range(2, G):
+            for k in range(4):
+                mx_pass(accs[k], 0, k, g)
 
         W2 = 2 * P
         qs = {}

@@ -197,7 +197,7 @@ def tile_ltccell_kernel(
 
         def a_bias(a, j):
             gt = work.tile([P, B], F32, name="gt", tag="gt", bufs=5)
-            nc.vector.tensor_scalar_add(out=gt[:], in0=a[:], scalar1=bias_c[:, j : j + 1])
+            nc.scalar.activation(out=gt[:], in_=a[:], func=ACT.Identity, bias=bias_c[:, j : j + 1], scale=1.0)
             return gt
 
         def turn_back(tiles, tag):
@@ -297,13 +297,18 @@ def tile_ltccell_kernel(
         ts = [f_lin(ys[k], k) for k in range(4)]
         for k in range(4):
             qs[k] = f_rate(ys[k], ts[k], k)
-        a_s = [a_tanh(acc_a[k], k) for k in range(4)]
         for k in range(4):
-            gts[k] = a_bias(a_s[k], k)
+            gts[k] = a_bias(a_tanh(acc_a[k], k), k)
+
+        def a_bias_v(a, j):
+            gt = work.tile([P, B], F32, name="gt", tag="gt", bufs=5)
+            nc.vector.tensor_scalar_add(out=gt[:], in0=a[:], scalar1=bias_c[:, j : j + 1])
+            return gt
 
         for i in range(1, NR):
             ua, ub = 2 * i, 2 * i + 1
             new = i >= 2
+            last = i == NR - 1
             if new:
                 acc_f = [group(0, ua), group(0, ub)]
             lo = W2 * (i - 1)
@@ -316,9 +321,9 @@ def tile_ltccell_kernel(
                 yb = f_abs(fb)
             dec = decay(q_banks)
             if new:
-                acc_a = [group(1, ua), group(1, ub)]
-                aa = a_tanh(acc_a[0], ua)
-                ab = a_tanh(acc_a[1], ub)
+                gts[ua] = a_bias(a_tanh(group(1, ua), ua), ua)
+                if not last:
+                    gts[ub] = a_bias(a_tanh(group(1, ub), ub), ub)
             mt, ot = b_tiles(W2)
             if new:
                 ta = f_lin(ya, ua)
@@ -331,27 +336,25 @@ def tile_ltccell_kernel(
             b_mul(mt, dec, 0, 2)
             if new:
                 qs[ub] = f_rate(yb, tb, ub)
+            if last:
+                dec_last = decay(turn_back([qs[ua], qs[ub]], "mx"))
+                a_last = a_tanh(group(1, ub), ub)
             b_mul(mt, dec, 2, 4)
-            if new:
-                gts[ua] = a_bias(aa, ua)
             b_add(ot, mt, lo, W2, 0, 2)
-            if new:
-                gts[ub] = a_bias(ab, ub)
             b_add(ot, mt, lo, W2, 2, 4)
             store(ot, lo, W2)
 
         ua, ub = NU - 2, NU - 1
-        q_banks = turn_back([qs[ua], qs[ub]], "t")
         bank_a = turn_back([gts[ua]], "t")
-        bank_b = turn_back([gts[ub]], "t")
-        dec = decay(q_banks)
         mt_a, ot_a = b_tiles(P)
         mt_b, ot_b = b_tiles(P)
+        gts[ub] = a_bias_v(a_last, ub)
+        bank_b = turn_back([gts[ub]], "t")
         b_sub(mt_a, P * ua, P, 0, 4, bank_a[0])
+        b_mul(mt_a, dec_last[:, :, 0:P], 0, 4)
         b_sub(mt_b, P * ub, P, 0, 4, bank_b[0])
-        b_mul(mt_a, dec[:, :, 0:P], 0, 4)
-        b_mul(mt_b, dec[:, :, P:W2], 0, 4)
         b_add(ot_a, mt_a, P * ua, P, 0, 4)
         store(ot_a, P * ua, P)
+        b_mul(mt_b, dec_last[:, :, P:W2], 0, 4)
         b_add(ot_b, mt_b, P * ub, P, 0, 4)
         store(ot_b, P * ub, P)

@@ -300,15 +300,9 @@ def tile_ltccell_kernel(
         for k in range(4):
             gts[k] = a_bias(a_tanh(acc_a[k], k), k)
 
-        def a_bias_v(a, j):
-            gt = work.tile([P, B], F32, name="gt", tag="gt", bufs=5)
-            nc.vector.tensor_scalar_add(out=gt[:], in0=a[:], scalar1=bias_c[:, j : j + 1])
-            return gt
-
         for i in range(1, NR):
             ua, ub = 2 * i, 2 * i + 1
             new = i >= 2
-            last = i == NR - 1
             if new:
                 acc_f = [group(0, ua), group(0, ub)]
             lo = W2 * (i - 1)
@@ -321,9 +315,9 @@ def tile_ltccell_kernel(
                 yb = f_abs(fb)
             dec = decay(q_banks)
             if new:
-                gts[ua] = a_bias(a_tanh(group(1, ua), ua), ua)
-                if not last:
-                    gts[ub] = a_bias(a_tanh(group(1, ub), ub), ub)
+                acc_a = [group(1, ua), group(1, ub)]
+                gts[ua] = a_bias(a_tanh(acc_a[0], ua), ua)
+                gts[ub] = a_bias(a_tanh(acc_a[1], ub), ub)
             mt, ot = b_tiles(W2)
             if new:
                 ta = f_lin(ya, ua)
@@ -336,25 +330,23 @@ def tile_ltccell_kernel(
             b_mul(mt, dec, 0, 2)
             if new:
                 qs[ub] = f_rate(yb, tb, ub)
-            if last:
-                dec_last = decay(turn_back([qs[ua], qs[ub]], "mx"))
-                a_last = a_tanh(group(1, ub), ub)
             b_mul(mt, dec, 2, 4)
             b_add(ot, mt, lo, W2, 0, 2)
             b_add(ot, mt, lo, W2, 2, 4)
             store(ot, lo, W2)
 
         ua, ub = NU - 2, NU - 1
+        q_banks = turn_back([qs[ua], qs[ub]], "t")
         bank_a = turn_back([gts[ua]], "t")
+        bank_b = turn_back([gts[ub]], "t")
+        dec = decay(q_banks)
         mt_a, ot_a = b_tiles(P)
         mt_b, ot_b = b_tiles(P)
-        gts[ub] = a_bias_v(a_last, ub)
-        bank_b = turn_back([gts[ub]], "t")
         b_sub(mt_a, P * ua, P, 0, 4, bank_a[0])
-        b_mul(mt_a, dec_last[:, :, 0:P], 0, 4)
         b_sub(mt_b, P * ub, P, 0, 4, bank_b[0])
+        b_mul(mt_a, dec[:, :, 0:P], 0, 4)
+        b_mul(mt_b, dec[:, :, P:W2], 0, 4)
         b_add(ot_a, mt_a, P * ua, P, 0, 4)
         store(ot_a, P * ua, P)
-        b_mul(mt_b, dec_last[:, :, P:W2], 0, 4)
         b_add(ot_b, mt_b, P * ub, P, 0, 4)
         store(ot_b, P * ub, P)

@@ -271,7 +271,7 @@ def tile_ltccell_kernel(
         for k in range(4):
             mx_pass(accs[k], 0, k, 1)
         c_pass(3)
-        nc.vector.tensor_copy(out=crow32[:], in_=crow[:])
+        nc.scalar.copy(out=crow32[:], in_=crow[:])
         c_pass(4)
         cps = psum.tile([P, 512], F32, name="cps", tag="t")
         nc.tensor.transpose(out=cps[:, 0:P], in_=crow32[:], identity=ident[:])

@@ -184,7 +184,7 @@ def tile_ltccell_kernel(
             return t
 
         def f_rate(y, t, j):
-            q = work.tile([P, B], F32, name="q", tag="q", bufs=5)
+            q = work.tile([P, B], F32, name="q", tag="q", bufs=8)
             nc.vector.scalar_tensor_tensor(
                 out=q[:], in0=y[:], scalar=itau[:, j : j + 1], in1=t[:], op0=ALU.add, op1=ALU.mult
             )
@@ -203,21 +203,18 @@ def tile_ltccell_kernel(
         def turn_back(tiles, tag):
             n = len(tiles)
             per_bank = 4 // n
-            banks = []
-            for b0 in range(0, NBT, per_bank):
-                bank = psum.tile([P, per_bank, n * P], F32, name="bank", tag=tag)
-                for t2 in range(per_bank):
-                    for k in range(n):
-                        nc.tensor.transpose(
-                            out=bank[:, t2, P * k : P * (k + 1)],
-                            in_=tiles[k][:, P * (b0 + t2) : P * (b0 + t2 + 1)],
-                            identity=ident[:],
-                        )
-                banks.append(bank)
+            banks = [psum.tile([P, per_bank, n * P], F32, name="bank", tag=tag) for b0 in range(0, NBT, per_bank)]
+            for k in range(n):
+                for bt in range(NBT):
+                    nc.tensor.transpose(
+                        out=banks[bt // per_bank][:, bt % per_bank, P * k : P * (k + 1)],
+                        in_=tiles[k][:, P * bt : P * (bt + 1)],
+                        identity=ident[:],
+                    )
             return banks
 
         def decay(banks):
-            dec = work.tile([P, NBT, 2 * P], F32, name="dec", tag="dec", bufs=2)
+            dec = work.tile([P, NBT, 2 * P], F32, name="dec", tag="dec", bufs=4)
             for bt in range(NBT):
                 nc.scalar.activation(
                     out=dec[:, bt, :], in_=banks[bt // 2][:, bt % 2, :], func=ACT.Exp, scale=ntd[:, bt : bt + 1]
@@ -291,62 +288,91 @@ def tile_ltccell_kernel(
         W2 = 2 * P
         qs = {}
         gts = {}
-        fs = [f_tanh(accs[k], k) for k in range(4)]
-        ys = [f_abs(fs[k]) for k in range(4)]
-        acc_a = [group(1, 0), group(1, 1), group(1, 2), group(1, 3)]
-        ts = [f_lin(ys[k], k) for k in range(4)]
-        for k in range(4):
-            qs[k] = f_rate(ys[k], ts[k], k)
-        for k in range(4):
-            gts[k] = a_bias(a_tanh(acc_a[k], k), k)
+        decs = {}
+        us = {}
 
-        for i in range(1, NR):
-            ua, ub = 2 * i, 2 * i + 1
-            new = i >= 2
-            if new:
-                acc_f = [group(0, ua), group(0, ub)]
-            lo = W2 * (i - 1)
-            q_banks = turn_back([qs[ua - 2], qs[ub - 2]], "t")
+        def f_scalar(r, accs_r):
+            return [f_abs(f_tanh(accs_r[e], 2 * r + e)) for e in range(2)]
+
+        def a_scalar(acc, j):
+            gts[j] = a_bias(a_tanh(acc, j), j)
+
+        def u_make(r):
+            u = work.tile([P, NBT, W2], F32, name="u", tag="u", bufs=4)
+            nc.vector.tensor_tensor(out=u[:], in0=decs[r][:], in1=h_part(W2 * r, W2, 0, NBT), op=ALU.mult)
+            us[r] = u
+
+        def p_make(pt, dec_view, t_lo, t_hi, bank):
+            nc.vector.scalar_tensor_tensor(
+                out=pt[:, t_lo:t_hi, :], in0=dec_view[:, t_lo:t_hi, :], scalar=1.0, in1=bank[:], op0=ALU.subtract, op1=ALU.mult
+            )
+
+        def o_make(ot, u_view, pt):
+            nc.vector.tensor_tensor(out=ot[:], in0=u_view, in1=pt[:], op=ALU.subtract)
+
+        ys = f_scalar(0, accs[0:2]) + f_scalar(1, accs[2:4])
+        acc_a = [group(1, 0), group(1, 1)]
+        acc_f = [group(0, 4), group(0, 5)]
+        for k0 in (0, 2):
+            ts = [f_lin(ys[k], k) for k in (k0, k0 + 1)]
+            for k in (k0, k0 + 1):
+                qs[k] = f_rate(ys[k], ts[k - k0], k)
+        a_scalar(acc_a[0], 0)
+        a_scalar(acc_a[1], 1)
+        ys = f_scalar(2, acc_f)
+        for r in range(2):
+            decs[r] = decay(turn_back([qs[2 * r], qs[2 * r + 1]], "t"))
+        ts = [f_lin(ys[e], 4 + e) for e in range(2)]
+        for e in range(2):
+            qs[4 + e] = f_rate(ys[e], ts[e], 4 + e)
+        u_make(0)
+        u_make(1)
+
+        for r in range(1, NR):
+            ua, ub = 2 * r, 2 * r + 1
+            va, vb = ua + 4, ub + 4
+            has_f = r + 2 < NR
+            has_q = r + 1 < NR
+            lo = W2 * (r - 1)
+            if has_f:
+                acc_f = [group(0, va), group(0, vb)]
+            else:
+                acc_a = [group(1, ua)]
+            if has_q:
+                q_banks = turn_back([qs[ua + 2], qs[ub + 2]], "t")
             g_banks = turn_back([gts[ua - 2], gts[ub - 2]], "t")
-            if new:
-                fa = f_tanh(acc_f[0], ua)
-                ya = f_abs(fa)
-                fb = f_tanh(acc_f[1], ub)
-                yb = f_abs(fb)
-            dec = decay(q_banks)
-            if new:
+            if has_f:
+                ys = f_scalar(r + 2, acc_f)
+            else:
+                a_scalar(acc_a[0], ua)
+            if has_q:
+                decs[r + 1] = decay(q_banks)
+            if has_f:
                 acc_a = [group(1, ua), group(1, ub)]
-                gts[ua] = a_bias(a_tanh(acc_a[0], ua), ua)
-                gts[ub] = a_bias(a_tanh(acc_a[1], ub), ub)
-            mt, ot = b_tiles(W2)
-            if new:
-                ta = f_lin(ya, ua)
-            b_sub(mt, lo, W2, 0, 2, g_banks[0])
-            if new:
-                tb = f_lin(yb, ub)
-            b_sub(mt, lo, W2, 2, 4, g_banks[1])
-            if new:
-                qs[ua] = f_rate(ya, ta, ua)
-            b_mul(mt, dec, 0, 2)
-            if new:
-                qs[ub] = f_rate(yb, tb, ub)
-            b_mul(mt, dec, 2, 4)
-            b_add(ot, mt, lo, W2, 0, 2)
-            b_add(ot, mt, lo, W2, 2, 4)
+                a_scalar(acc_a[0], ua)
+            else:
+                acc_a.append(group(1, ub))
+            a_scalar(acc_a[1], ub)
+            pt, ot = b_tiles(W2)
+            if has_f:
+                ta = f_lin(ys[0], va)
+            p_make(pt, decs[r - 1], 0, 2, g_banks[0])
+            if has_f:
+                tb = f_lin(ys[1], vb)
+            p_make(pt, decs[r - 1], 2, 4, g_banks[1])
+            if has_f:
+                qs[va] = f_rate(ys[0], ta, va)
+                qs[vb] = f_rate(ys[1], tb, vb)
+            o_make(ot, us[r - 1][:], pt)
             store(ot, lo, W2)
+            if has_q:
+                u_make(r + 1)
 
-        ua, ub = NU - 2, NU - 1
-        q_banks = turn_back([qs[ua], qs[ub]], "t")
-        bank_a = turn_back([gts[ua]], "t")
-        bank_b = turn_back([gts[ub]], "t")
-        dec = decay(q_banks)
-        mt_a, ot_a = b_tiles(P)
-        mt_b, ot_b = b_tiles(P)
-        b_sub(mt_a, P * ua, P, 0, 4, bank_a[0])
-        b_sub(mt_b, P * ub, P, 0, 4, bank_b[0])
-        b_mul(mt_a, dec[:, :, 0:P], 0, 4)
-        b_mul(mt_b, dec[:, :, P:W2], 0, 4)
-        b_add(ot_a, mt_a, P * ua, P, 0, 4)
-        store(ot_a, P * ua, P)
-        b_add(ot_b, mt_b, P * ub, P, 0, 4)
-        store(ot_b, P * ub, P)
+        r = NR - 1
+        for e in range(2):
+            j = 2 * r + e
+            bank = turn_back([gts[j]], "t")[0]
+            pt, ot = b_tiles(P)
+            p_make(pt, decs[r][:, :, P * e : P * (e + 1)], 0, NBT, bank)
+            o_make(ot, us[r][:, :, P * e : P * (e + 1)], pt)
+            store(ot, P * j, P)

@@ -350,9 +350,10 @@ def tile_ltccell_kernel(
             if has_f:
                 acc_a = [group(1, ua), group(1, ub)]
                 a_scalar(acc_a[0], ua)
-            else:
+            elif r < NR - 1:
                 acc_a.append(group(1, ub))
-            a_scalar(acc_a[1], ub)
+            if r < NR - 1:
+                a_scalar(acc_a[1], ub)
             pt, ot = b_tiles(W2)
             if has_f:
                 ta = f_lin(ys[0], va)
@@ -369,10 +370,57 @@ def tile_ltccell_kernel(
                 u_make(r + 1)
 
         r = NR - 1
-        for e in range(2):
-            j = 2 * r + e
-            bank = turn_back([gts[j]], "t")[0]
-            pt, ot = b_tiles(P)
-            p_make(pt, decs[r][:, :, P * e : P * (e + 1)], 0, NBT, bank)
-            o_make(ot, us[r][:, :, P * e : P * (e + 1)], pt)
-            store(ot, P * j, P)
+        ja, jb = NU - 2, NU - 1
+        a_q = work.tile([P, B], F32, name="a", tag="a", bufs=4)
+        g_q = work.tile([P, B], F32, name="gt", tag="gt", bufs=5)
+        pt_a, ot_a = b_tiles(P)
+        pt_b, ot_b = b_tiles(P)
+
+        def quarter_mx(bt):
+            acc = psum.tile([P, P], F32, name="acc_q", tag="mx")
+            cols = slice(P * bt, P * (bt + 1))
+            for g in range(G):
+                nc.tensor.matmul_mx(
+                    out=acc[:],
+                    lhsT=w_t[1][jb // 4][:, g, 2 * P * (jb % 4) : 2 * P * (jb % 4 + 1)].bitcast(FP4X4),
+                    lhsT_scale=pl_b[1][:, g, P * (jb - 4) : P * (jb - 3)],
+                    rhs=codes[:, g, cols].bitcast(FP8X4),
+                    rhs_scale=cpl[:, g, cols],
+                    start=(g == 0),
+                    stop=(g == G - 1),
+                )
+            nc.scalar.activation(out=a_q[:, cols], in_=acc[:], func=ACT.Tanh, bias=bt_[:, jb : jb + 1], scale=1.0)
+            nc.scalar.activation(out=g_q[:, cols], in_=a_q[:, cols], func=ACT.Identity, bias=bias_c[:, jb : jb + 1], scale=1.0)
+
+        def quarter_out(bt):
+            bank = psum.tile([P, P], F32, name="bank_q", tag="t")
+            nc.tensor.transpose(out=bank[:], in_=g_q[:, P * bt : P * (bt + 1)], identity=ident[:])
+            nc.vector.scalar_tensor_tensor(
+                out=pt_b[:, bt, :], in0=decs[r][:, bt, P:W2], scalar=1.0, in1=bank[:], op0=ALU.subtract, op1=ALU.mult
+            )
+            return bt
+
+        def quarter_end(bt):
+            nc.vector.tensor_tensor(out=ot_b[:, bt, :], in0=us[r][:, bt, P:W2], in1=pt_b[:, bt, :], op=ALU.subtract)
+            nc.sync.dma_start(out=out_dst[:, bt, P * jb : P * (jb + 1)], in_=ot_b[:, bt, :])
+
+        def unit_a():
+            bank = turn_back([gts[ja]], "t")[0]
+            p_make(pt_a, decs[r][:, :, 0:P], 0, NBT, bank)
+
+        def unit_a_end():
+            o_make(ot_a, us[r][:, :, 0:P], pt_a)
+            store(ot_a, P * ja, P)
+
+        for bt in range(NBT):
+            quarter_mx(bt)
+        unit_a()
+        quarter_out(0)
+        unit_a_end()
+        quarter_out(1)
+        quarter_end(0)
+        quarter_out(2)
+        quarter_end(1)
+        quarter_out(3)
+        quarter_end(2)
+        quarter_end(3)

@@ -294,6 +294,11 @@ def tile_ltccell_kernel(
         def f_scalar(r, accs_r):
             return [f_abs(f_tanh(accs_r[e], 2 * r + e)) for e in range(2)]
 
+        def a_bias_v(a, j):
+            gt = work.tile([P, B], F32, name="gt", tag="gt", bufs=5)
+            nc.vector.tensor_scalar_add(out=gt[:], in0=a[:], scalar1=bias_c[:, j : j + 1])
+            return gt
+
         def a_scalar(acc, j):
             gts[j] = a_bias(a_tanh(acc, j), j)
 
@@ -317,11 +322,12 @@ def tile_ltccell_kernel(
             ts = [f_lin(ys[k], k) for k in (k0, k0 + 1)]
             for k in (k0, k0 + 1):
                 qs[k] = f_rate(ys[k], ts[k - k0], k)
-        a_scalar(acc_a[0], 0)
-        a_scalar(acc_a[1], 1)
+        a_early = [a_tanh(acc_a[e], e) for e in range(2)]
         ys = f_scalar(2, acc_f)
         for r in range(2):
             decs[r] = decay(turn_back([qs[2 * r], qs[2 * r + 1]], "t"))
+        for e in range(2):
+            gts[e] = a_bias_v(a_early[e], e)
         ts = [f_lin(ys[e], 4 + e) for e in range(2)]
         for e in range(2):
             qs[4 + e] = f_rate(ys[e], ts[e], 4 + e)

@@ -22,7 +22,7 @@ NU = H // P
 NR = NU // 2
 EPS = 1e-6
 WARM_HEAD = 8
-WARM_GAP = 3
+WARM_GAP = 0
 
 FLOPS = 2 * 2 * B * K * H
 

from contextlib import ExitStack

import concourse.mybir as mybir
from concourse.masks import make_identity

F32 = mybir.dt.float32
BF16 = mybir.dt.bfloat16
I32 = mybir.dt.int32
U32 = mybir.dt.uint32
U8 = mybir.dt.uint8
FP8X4 = mybir.dt.float8_e4m3fn_x4
FP4X4 = mybir.dt.float4_e2m1fn_x4
ACT = mybir.ActivationFunctionType
ALU = mybir.AluOpType

P = 128
B, I, H = 512, 512, 2048
K = I + H
G = K // 512
NBT = B // P
NU = H // P
NR = NU // 2
EPS = 1e-6
WARM_HEAD = 8
WARM_GAP = 0

FLOPS = 2 * 2 * B * K * H


def tile_ltccell_kernel(
    tc, x, h, time_delta, W_mod_words, W_mod_scales, b_mod, W_tgt_words, W_tgt_scales, b_tgt, log_tau, bias, out
):
    nc = tc.nc
    with ExitStack() as ctx:
        ctx.enter_context(tc.manual_schedule())
        keep = ctx.enter_context(tc.tile_pool(name="keep", bufs=1))
        stage = ctx.enter_context(tc.tile_pool(name="stage", bufs=2))
        work = ctx.enter_context(tc.tile_pool(name="work", bufs=2))
        psum = ctx.enter_context(tc.psum_pool(name="psum", bufs=4))

        x_t = [keep.tile([P, 2, 512], BF16, name="x_t%d" % half, align_bytes=64) for half in range(2)]
        c_t = [None] + [keep.tile([P, NBT, 512], BF16, name="c_t%d" % g, align_bytes=64) for g in range(1, G)]
        w_t = [
            [keep.tile([P, G, 1024], U8, name="w_t%d_%d" % (m, blk), align_bytes=64) for blk in range(4)]
            for m in range(2)
        ]
        pl_a = [keep.tile([P, G, 512], U8, name="pl_a%d" % m, align_bytes=64) for m in range(2)]
        pl_b = [keep.tile([P, G, H - 512], U8, name="pl_b%d" % m, align_bytes=64) for m in range(2)]
        codes = keep.tile([P, G, B], U32, name="codes", align_bytes=64)
        cpl = keep.tile([P, G, B], U8, name="cpl", align_bytes=64)
        ident = keep.tile([P, P], F32, name="ident")
        crow = keep.tile([P, P], BF16, name="crow")
        crow32 = keep.tile([P, P], F32, name="crow32")
        cst = keep.tile([P, P], F32, name="cst")
        ltc = keep.tile([P, NU], F32, name="ltc")
        itau = keep.tile([P, NU], F32, name="itau")
        c1 = keep.tile([P, NU], F32, name="c1")
        arec = keep.tile([P, NU], F32, name="arec")
        nbk = keep.tile([P, NU], F32, name="nbk")
        ntd = keep.tile([P, NBT], F32, name="ntd")
        warm_in = keep.tile([P, 1], F32, name="warm_in")
        warm_out = keep.tile([P, 1], F32, name="warm_out")
        zeros = keep.tile([P, 512], BF16, name="zeros")

        words = [W_mod_words, W_tgt_words]
        scales = [W_mod_scales, W_tgt_scales]
        w_src = [w.bitcast(I32).rearrange("g p w -> p g w") for w in words]
        s_src = [s.bitcast(I32).rearrange("g q n -> q g n") for s in scales]
        h_src = h.rearrange("(t p) k -> p t k", p=P)
        out_dst = out.rearrange("(t p) n -> p t n", p=P)

        def load_words(m, blk, g_lo=0, g_hi=G):
            lo, hi = 256 * blk, 256 * (blk + 1)
            nc.sync.dma_start(out=w_t[m][blk][:].bitcast(I32)[:, g_lo:g_hi, :], in_=w_src[m][:, g_lo:g_hi, lo:hi])

        def load_scales(m, first):
            plane = pl_a[m] if first else pl_b[m]
            lo, hi = (0, 128) if first else (128, 512)
            for r in range(4):
                nc.sync.dma_start(out=plane[:].bitcast(I32)[r:P:32, :, :], in_=s_src[m][r:16:4, :, lo:hi])

        def load_h(g):
            nc.sync.dma_start(out=c_t[g][:], in_=h_src[:, :, 512 * (g - 1) : 512 * g])

        nc.vector.memset(zeros[:], 0.0)
        nc.vector.memset(warm_in[:], 0.0)
        nc.scalar.activation(out=warm_out[:], in_=warm_in[:], func=ACT.Tanh)
        nc.vector.memset(pl_a[0][:].bitcast(I32), 0)
        nc.vector.memset(crow[:], 0.0)
        nc.vector.memset(pl_a[1][:].bitcast(I32), 0)
        nc.vector.memset(pl_b[0][:].bitcast(I32), 0)
        nc.vector.memset(pl_b[1][:].bitcast(I32), 0)
        make_identity(nc, ident[:])

        x_src = x.rearrange("(t p) k -> p t k", p=P)
        for half in range(2):
            nc.sync.dma_start(out=x_t[half][:], in_=x_src[:, 2 * half : 2 * half + 2, :])
        load_h(1)
        load_scales(0, True)
        load_words(0, 0, 0, 1)
        load_h(2)
        load_words(0, 0, 1, G)
        load_h(3)
        load_h(4)
        for i, vec in enumerate([b_mod, b_tgt, log_tau, bias]):
            nc.sync.dma_start(out=crow[NU * i : NU * (i + 1), :], in_=vec.rearrange("(j p) -> j p", p=P))
        nc.sync.dma_start(out=crow[4 * NU : 4 * NU + NBT, :], in_=time_delta.rearrange("(t p) o -> t (p o)", p=P))
        load_scales(1, True)
        load_words(1, 0)
        load_scales(0, False)
        load_words(0, 1)
        load_scales(1, False)
        load_words(1, 1)
        for blk in range(2, 4):
            load_words(0, blk)
            load_words(1, blk)

        bm = cst[:, 0:NU]
        bt_ = cst[:, NU : 2 * NU]
        bias_c = cst[:, 3 * NU : 4 * NU]

        def c_pass(g):
            grp = stage.tile([P, 4 * B], BF16, name="grp", tag="grp", align_bytes=64)
            grp32 = grp[:].bitcast(F32).rearrange("p (b u) -> p b u", u=2)
            for half in range(2):
                ct = psum.tile([P, 2, 256], F32, name="ct", tag="t")
                for t2 in range(2):
                    rows = x_t[half][:, t2, :] if g == 0 else c_t[g][:, 2 * half + t2, :]
                    cw = rows.bitcast(F32)
                    for u in range(2):
                        nc.tensor.transpose(
                            out=ct[:, u, P * t2 : P * (t2 + 1)],
                            in_=cw[:, u:256:2],
                            identity=ident[:],
                        )
                dst = grp32[:, 256 * half : 256 * (half + 1), :]
                src = ct[:].rearrange("p u b -> p b u")
                if half == 0:
                    nc.scalar.copy(out=dst, in_=src)
                else:
                    nc.vector.tensor_copy(out=dst, in_=src)
            nc.vector.quantize_mx(out=codes[:, g, :].bitcast(FP8X4), scales=cpl[:, g, :], in_=grp[:])

        def mx_pass(acc, m, j, g):
            if j < 4:
                plane = pl_a[m][:, g, P * j : P * (j + 1)]
            else:
                plane = pl_b[m][:, g, P * (j - 4) : P * (j - 3)]
            nc.tensor.matmul_mx(
                out=acc[:],
                lhsT=w_t[m][j // 4][:, g, 2 * P * (j % 4) : 2 * P * (j % 4 + 1)].bitcast(FP4X4),
                lhsT_scale=plane,
                rhs=codes[:, g, :].bitcast(FP8X4),
                rhs_scale=cpl[:, g, :],
                start=(g == 0),
                stop=(g == G - 1),
            )

        def new_acc():
            acc = psum.tile([P, B], F32, name="acc", tag="mx")
            return acc

        def group(m, j):
            acc = new_acc()
            for g in range(G):
                mx_pass(acc, m, j, g)
            return acc

        def f_tanh(acc, j):
            f = work.tile([P, B], F32, name="f", tag="f", bufs=4)
            nc.scalar.activation(out=f[:], in_=acc[:], func=ACT.Tanh, bias=bm[:, j : j + 1], scale=1.0)
            return f

        def f_abs(f):
            y = work.tile([P, B], F32, name="y", tag="y", bufs=4)
            nc.scalar.activation(out=y[:], in_=f[:], func=ACT.Abs)
            return y

        def f_lin(y, j):
            t = work.tile([P, B], F32, name="t", tag="t", bufs=4)
            nc.vector.tensor_scalar(
                out=t[:], in0=y[:], scalar1=nbk[:, j : j + 1], scalar2=arec[:, j : j + 1], op0=ALU.mult, op1=ALU.add
            )
            return t

        def f_rate(y, t, j):
            q = work.tile([P, B], F32, name="q", tag="q", bufs=8)
            nc.vector.scalar_tensor_tensor(
                out=q[:], in0=y[:], scalar=itau[:, j : j + 1], in1=t[:], op0=ALU.add, op1=ALU.mult
            )
            return q

        def a_tanh(acc, j):
            a = work.tile([P, B], F32, name="a", tag="a", bufs=4)
            nc.scalar.activation(out=a[:], in_=acc[:], func=ACT.Tanh, bias=bt_[:, j : j + 1], scale=1.0)
            return a

        def a_bias(a, j):
            gt = work.tile([P, B], F32, name="gt", tag="gt", bufs=5)
            nc.scalar.activation(out=gt[:], in_=a[:], func=ACT.Identity, bias=bias_c[:, j : j + 1], scale=1.0)
            return gt

        def turn_back(tiles, tag):
            n = len(tiles)
            per_bank = 4 // n
            banks = [psum.tile([P, per_bank, n * P], F32, name="bank", tag=tag) for b0 in range(0, NBT, per_bank)]
            for k in range(n):
                for bt in range(NBT):
                    nc.tensor.transpose(
                        out=banks[bt // per_bank][:, bt % per_bank, P * k : P * (k + 1)],
                        in_=tiles[k][:, P * bt : P * (bt + 1)],
                        identity=ident[:],
                    )
            return banks

        def decay(banks):
            dec = work.tile([P, NBT, 2 * P], F32, name="dec", tag="dec", bufs=4)
            for bt in range(NBT):
                nc.scalar.activation(
                    out=dec[:, bt, :], in_=banks[bt // 2][:, bt % 2, :], func=ACT.Exp, scale=ntd[:, bt : bt + 1]
                )
            return dec

        def h_part(lo, width, t_lo, t_hi):
            return c_t[1 + lo // 512][:, t_lo:t_hi, lo % 512 : lo % 512 + width]

        def b_sub(mt, lo, width, t_lo, t_hi, bank):
            nc.vector.tensor_tensor(
                out=mt[:, t_lo:t_hi, :], in0=h_part(lo, width, t_lo, t_hi), in1=bank[:], op=ALU.subtract
            )

        def b_mul(mt, dec_view, t_lo, t_hi):
            nc.vector.scalar_tensor_tensor(
                out=mt[:, t_lo:t_hi, :],
                in0=dec_view[:, t_lo:t_hi, :],
                scalar=1.0,
                in1=mt[:, t_lo:t_hi, :],
                op0=ALU.subtract,
                op1=ALU.mult,
            )

        def b_add(ot, mt, lo, width, t_lo, t_hi):
            nc.vector.tensor_tensor(
                out=ot[:, t_lo:t_hi, :], in0=h_part(lo, width, t_lo, t_hi), in1=mt[:, t_lo:t_hi, :], op=ALU.add
            )

        def b_tiles(width):
            mt = work.tile([P, NBT, width], F32, name="mt%d" % width, tag="mt%d" % width, bufs=2)
            ot = work.tile([P, NBT, width], F32, name="ot%d" % width, tag="ot%d" % width, bufs=3)
            return mt, ot

        def store(ot, lo, width):
            nc.sync.dma_start(out=out_dst[:, :, lo : lo + width], in_=ot[:])

        def idle_passes(n):
            for k in range(n):
                nc.tensor.matmul(out=spare[:], lhsT=zeros[:, 0:P], rhs=zeros[:], start=True, stop=True)

        spare = new_acc()
        idle_passes(WARM_HEAD)
        c_pass(0)
        idle_passes(WARM_GAP)
        c_pass(1)
        accs = [new_acc() for k in range(4)]
        for k in range(4):
            mx_pass(accs[k], 0, k, 0)
        c_pass(2)
        for k in range(4):
            mx_pass(accs[k], 0, k, 1)
        c_pass(3)
        nc.scalar.copy(out=crow32[:], in_=crow[:])
        c_pass(4)
        cps = psum.tile([P, 512], F32, name="cps", tag="t")
        nc.tensor.transpose(out=cps[:, 0:P], in_=crow32[:], identity=ident[:])
        nc.vector.tensor_copy(out=cst[:], in_=cps[:, 0:P])
        nc.vector.tensor_scalar_max(out=ltc[:], in0=cst[:, 2 * NU : 3 * NU], scalar1=-60.0)
        nc.scalar.activation(out=itau[:], in_=ltc[:], func=ACT.Exp, scale=-1.0)
        nc.vector.tensor_scalar(out=c1[:], in0=itau[:], scalar1=EPS, scalar2=1.0, op0=ALU.mult, op1=ALU.add)
        nc.vector.reciprocal(out=arec[:], in_=c1[:])
        nc.vector.scalar_tensor_tensor(
            out=nbk[:], in0=arec[:], scalar=-EPS, in1=arec[:], op0=ALU.mult, op1=ALU.mult
        )
        nc.vector.tensor_scalar_mul(out=ntd[:], in0=cst[:, 4 * NU : 4 * NU + NBT], scalar1=-1.0)
        for g in range(2, G):
            for k in range(4):
                mx_pass(accs[k], 0, k, g)

        W2 = 2 * P
        qs = {}
        gts = {}
        decs = {}
        us = {}

        def f_scalar(r, accs_r):
            return [f_abs(f_tanh(accs_r[e], 2 * r + e)) for e in range(2)]

        def a_bias_v(a, j):
            gt = work.tile([P, B], F32, name="gt", tag="gt", bufs=5)
            nc.vector.tensor_scalar_add(out=gt[:], in0=a[:], scalar1=bias_c[:, j : j + 1])
            return gt

        def a_scalar(acc, j):
            gts[j] = a_bias(a_tanh(acc, j), j)

        def u_make(r):
            u = work.tile([P, NBT, W2], F32, name="u", tag="u", bufs=4)
            nc.vector.tensor_tensor(out=u[:], in0=decs[r][:], in1=h_part(W2 * r, W2, 0, NBT), op=ALU.mult)
            us[r] = u

        def p_make(pt, dec_view, t_lo, t_hi, bank):
            nc.vector.scalar_tensor_tensor(
                out=pt[:, t_lo:t_hi, :], in0=dec_view[:, t_lo:t_hi, :], scalar=1.0, in1=bank[:], op0=ALU.subtract, op1=ALU.mult
            )

        def o_make(ot, u_view, pt):
            nc.vector.tensor_tensor(out=ot[:], in0=u_view, in1=pt[:], op=ALU.subtract)

        ys = f_scalar(0, accs[0:2]) + f_scalar(1, accs[2:4])
        acc_a = [group(1, 0), group(1, 1)]
        acc_f = [group(0, 4), group(0, 5)]
        for k0 in (0, 2):
            ts = [f_lin(ys[k], k) for k in (k0, k0 + 1)]
            for k in (k0, k0 + 1):
                qs[k] = f_rate(ys[k], ts[k - k0], k)
        a_early = [a_tanh(acc_a[e], e) for e in range(2)]
        ys = f_scalar(2, acc_f)
        for r in range(2):
            decs[r] = decay(turn_back([qs[2 * r], qs[2 * r + 1]], "t"))
        for e in range(2):
            gts[e] = a_bias_v(a_early[e], e)
        ts = [f_lin(ys[e], 4 + e) for e in range(2)]
        for e in range(2):
            qs[4 + e] = f_rate(ys[e], ts[e], 4 + e)
        u_make(0)
        u_make(1)

        for r in range(1, NR):
            ua, ub = 2 * r, 2 * r + 1
            va, vb = ua + 4, ub + 4
            has_f = r + 2 < NR
            has_q = r + 1 < NR
            lo = W2 * (r - 1)
            if has_f:
                acc_f = [group(0, va), group(0, vb)]
            else:
                acc_a = [group(1, ua)]
            if has_q:
                q_banks = turn_back([qs[ua + 2], qs[ub + 2]], "t")
            g_banks = turn_back([gts[ua - 2], gts[ub - 2]], "t")
            if has_f:
                ys = f_scalar(r + 2, acc_f)
            else:
                a_scalar(acc_a[0], ua)
            if has_q:
                decs[r + 1] = decay(q_banks)
            if has_f:
                acc_a = [group(1, ua), group(1, ub)]
                a_scalar(acc_a[0], ua)
            elif r < NR - 1:
                acc_a.append(group(1, ub))
            if r < NR - 1:
                a_scalar(acc_a[1], ub)
            pt, ot = b_tiles(W2)
            if has_f:
                ta = f_lin(ys[0], va)
            p_make(pt, decs[r - 1], 0, 2, g_banks[0])
            if has_f:
                tb = f_lin(ys[1], vb)
            p_make(pt, decs[r - 1], 2, 4, g_banks[1])
            if has_f:
                qs[va] = f_rate(ys[0], ta, va)
                qs[vb] = f_rate(ys[1], tb, vb)
            o_make(ot, us[r - 1][:], pt)
            store(ot, lo, W2)
            if has_q:
                u_make(r + 1)

        r = NR - 1
        ja, jb = NU - 2, NU - 1
        a_q = work.tile([P, B], F32, name="a", tag="a", bufs=4)
        g_q = work.tile([P, B], F32, name="gt", tag="gt", bufs=5)
        pt_a, ot_a = b_tiles(P)
        pt_b, ot_b = b_tiles(P)

        def quarter_mx(bt):
            acc = psum.tile([P, P], F32, name="acc_q", tag="mx")
            cols = slice(P * bt, P * (bt + 1))
            for g in range(G):
                nc.tensor.matmul_mx(
                    out=acc[:],
                    lhsT=w_t[1][jb // 4][:, g, 2 * P * (jb % 4) : 2 * P * (jb % 4 + 1)].bitcast(FP4X4),
                    lhsT_scale=pl_b[1][:, g, P * (jb - 4) : P * (jb - 3)],
                    rhs=codes[:, g, cols].bitcast(FP8X4),
                    rhs_scale=cpl[:, g, cols],
                    start=(g == 0),
                    stop=(g == G - 1),
                )
            nc.scalar.activation(out=a_q[:, cols], in_=acc[:], func=ACT.Tanh, bias=bt_[:, jb : jb + 1], scale=1.0)
            nc.scalar.activation(out=g_q[:, cols], in_=a_q[:, cols], func=ACT.Identity, bias=bias_c[:, jb : jb + 1], scale=1.0)

        def quarter_out(bt):
            bank = psum.tile([P, P], F32, name="bank_q", tag="t")
            nc.tensor.transpose(out=bank[:], in_=g_q[:, P * bt : P * (bt + 1)], identity=ident[:])
            nc.vector.scalar_tensor_tensor(
                out=pt_b[:, bt, :], in0=decs[r][:, bt, P:W2], scalar=1.0, in1=bank[:], op0=ALU.subtract, op1=ALU.mult
            )
            return bt

        def quarter_end(bt):
            nc.vector.tensor_tensor(out=ot_b[:, bt, :], in0=us[r][:, bt, P:W2], in1=pt_b[:, bt, :], op=ALU.subtract)
            nc.sync.dma_start(out=out_dst[:, bt, P * jb : P * (jb + 1)], in_=ot_b[:, bt, :])

        def unit_a():
            bank = turn_back([gts[ja]], "t")[0]
            p_make(pt_a, decs[r][:, :, 0:P], 0, NBT, bank)

        def unit_a_end():
            o_make(ot_a, us[r][:, :, 0:P], pt_a)
            store(ot_a, P * ja, P)

        for bt in range(NBT):
            quarter_mx(bt)
        unit_a()
        quarter_out(0)
        unit_a_end()
        quarter_out(1)
        quarter_end(0)
        quarter_out(2)
        quarter_end(1)
        quarter_out(3)
        quarter_end(2)
        quarter_end(3)
